import numpy as np
import ml_dtypes


def mxq(x, axis, fmt="e4m3"):
    dtype, down = {"e4m3": (ml_dtypes.float8_e4m3fn, 7), "e5m2": (ml_dtypes.float8_e5m2, 14)}[fmt]
    v = np.moveaxis(np.asarray(x, np.float32).astype(ml_dtypes.bfloat16).astype(np.float64), axis, -1)
    blocks = v.reshape(v.shape[:-1] + (-1, 32))
    amax = np.abs(blocks).max(-1, keepdims=True)
    byte = np.maximum(np.where(amax > 0, np.frexp(amax)[1] - 1 + 127, 0) - down, 1)
    scale = np.exp2(byte - 127.0)
    codes = (blocks / scale).astype(np.float32).astype(dtype).astype(np.float64)
    return np.moveaxis((codes * scale).reshape(v.shape), -1, axis)


WIDE = False


def mx_kscale(k):
    if not WIDE:
        return np.ones(k)
    levels = np.array([10, -10, 5, -5, 0])
    a = np.random.permutation(np.resize(levels, k // 512 * 4)).reshape(k // 512, 4)
    idx = np.arange(k)
    return np.exp2(a[idx // 512, idx % 128 // 32])


BF16 = ml_dtypes.bfloat16


def bf(x):
    return np.asarray(x, np.float32).astype(BF16)


def f64(x):
    return np.asarray(x).astype(np.float64)


E2M1 = np.array([0.0, 0.5, 1.0, 1.5, 2.0, 3.0, 4.0, 6.0, -0.0, -0.5, -1.0, -1.5, -2.0, -3.0, -4.0, -6.0])


def pack_weight(w, fmt):
    k, n = w.shape
    w = f64(bf(w)).reshape(k // 32, 32, n)
    amax = np.abs(w).max(1)
    if fmt == "e4m3":
        byte = np.frexp(amax)[1] - 1 + 127 - 7
    else:
        mant, ex = np.frexp(amax / 6.0)
        byte = np.where(mant > 0.5, ex, ex - 1) + 127
    byte = np.clip(np.where(amax > 0, byte, 1), 1, 254)
    scaled = (w * np.exp2(127.0 - byte)[:, None, :]).reshape(k, n).astype(np.float32)
    by_word = np.ascontiguousarray(scaled.reshape(k // 512, 128, 4, n).transpose(0, 1, 3, 2))
    if fmt == "e4m3":
        words = by_word.astype(ml_dtypes.float8_e4m3fn).view(np.uint8)
    else:
        c = by_word.astype(ml_dtypes.float4_e2m1fn).view(np.uint8) & 0xF
        words = c[..., 0::2] | (c[..., 1::2] << 4)
    return np.ascontiguousarray(words), np.ascontiguousarray(byte.astype(np.uint8).reshape(k // 512, 16, n))


def unpack_weight(words, scales, fmt):
    g, p, n, _ = words.shape
    if fmt == "e4m3":
        vals = np.ascontiguousarray(words).view(ml_dtypes.float8_e4m3fn).astype(np.float64)
    else:
        nib = np.empty((g, p, n, 4), np.uint8)
        nib[..., 0::2] = words & 0xF
        nib[..., 1::2] = words >> 4
        vals = E2M1[nib]
    vals = vals * np.repeat(np.exp2(scales.astype(np.float64) - 127.0), 8, axis=1)[..., None]
    return vals.transpose(0, 1, 3, 2).reshape(g * 512, n)

def pack4(w):
    words, scales = pack_weight(w, "e2m1")
    return words.reshape(words.shape[0], 128, -1), scales


def unpack4(words, scales):
    return unpack_weight(words.reshape(words.shape[0], 128, -1, 2), scales, "e2m1")


B, L, F, D, N = 64, 32, 512, 256, 8192
TOP = 0.8 * np.sqrt(2.0 * np.log(L))


def elu(v):
    return np.where(v > 0.0, v, np.exp(np.minimum(v, 0.0)) - 1.0)


def setup_inputs():
    s = mx_kscale(F)
    x = bf(np.random.standard_normal((B, L, F)) * s)
    words, scales = pack4((np.random.standard_normal((D, F)) / np.sqrt(F) / s).T)
    conv_b = bf(np.random.standard_normal(D) * 2.0 - TOP)
    return {"x": x,
            "conv_w_words": words,
            "conv_w_scales": scales,
            "conv_b": conv_b}


def reference(x, conv_w_words, conv_w_scales, conv_b):
    z = (mxq(f64(x), 2, "e4m3") @ unpack4(conv_w_words, conv_w_scales)) + f64(conv_b)
    return elu(z).max(axis=1)

@@ -1,0 +1,138 @@
+from contextlib import ExitStack
+
+import concourse.masks as masks
+import concourse.mybir as mybir
+
+F32 = mybir.dt.float32
+BF16 = mybir.dt.bfloat16
+I32 = mybir.dt.int32
+U32 = mybir.dt.uint32
+U8 = mybir.dt.uint8
+FP8X4 = mybir.dt.float8_e4m3fn_x4
+FP4X4 = mybir.dt.float4_e2m1fn_x4
+ALU = mybir.AluOpType
+ACT = mybir.ActivationFunctionType
+
+P = 128
+PACK = 4
+SEQS = 64
+POSITIONS = 32
+FEATURES = 512
+CHANNELS = 256
+ROWS = SEQS * POSITIONS
+HALVES = CHANNELS // P
+WORDS_PER_ROW = FEATURES // 2
+PAIRS = PACK // 2
+BANK_F32 = 512
+ROWS_PER_PARTITION = BANK_F32 // WORDS_PER_ROW
+CHUNK_ROWS = P * ROWS_PER_PARTITION
+CHUNKS = ROWS // CHUNK_ROWS
+CHUNK_SEQS = CHUNK_ROWS // POSITIONS
+SCALE_ROWS_PER_QUADRANT = 4
+
+FLOPS = 2 * ROWS * FEATURES * CHANNELS
+
+
+def tile_conceptembedmodel_pa_s_kernel(tc, x, conv_w_words, conv_w_scales, conv_b, out):
+    nc = tc.nc
+    assert tuple(x.shape) == (SEQS, POSITIONS, FEATURES)
+    assert FEATURES == P * PACK, "the contraction is one matmul_mx pass"
+    x_rows = x.rearrange("b l f -> (b l) f")
+
+    with ExitStack() as ctx:
+        keep = ctx.enter_context(tc.tile_pool(name="keep", bufs=1))
+        loads = ctx.enter_context(tc.tile_pool(name="loads", bufs=CHUNKS))
+        stage = ctx.enter_context(tc.tile_pool(name="stage", bufs=3))
+        psum_t = ctx.enter_context(tc.psum_pool(name="psum_t", bufs=3))
+        psum_z = ctx.enter_context(tc.psum_pool(name="psum_z", bufs=3))
+        psum_end = ctx.enter_context(tc.psum_pool(name="psum_end", bufs=1))
+
+        def load_chunk(c):
+            x_chunk = loads.tile([P, ROWS_PER_PARTITION * FEATURES], BF16)
+            nc.sync.dma_start(
+                out=x_chunk[:],
+                in_=x_rows[c * CHUNK_ROWS : (c + 1) * CHUNK_ROWS, :].rearrange(
+                    "(r t) f -> r (t f)", t=ROWS_PER_PARTITION
+                ),
+            )
+            return x_chunk
+
+        x_chunks = [load_chunk(0), load_chunk(1)]
+
+        w_words = keep.tile([P, 2 * CHANNELS], U8, align_bytes=64)
+        nc.sync.dma_start(out=w_words[:].bitcast(I32), in_=conv_w_words[0].bitcast(I32))
+        w_scales = keep.tile([P, CHANNELS], U8, align_bytes=64)
+        nc.vector.memset(w_scales[:].bitcast(I32), 0)
+        for quadrant in range(P // 32):
+            first = SCALE_ROWS_PER_QUADRANT * quadrant
+            nc.sync.dma_start(
+                out=w_scales[32 * quadrant : 32 * quadrant + SCALE_ROWS_PER_QUADRANT, :].bitcast(I32),
+                in_=conv_w_scales[0, first : first + SCALE_ROWS_PER_QUADRANT, :].bitcast(I32),
+            )
+
+        for c in range(2, CHUNKS):
+            x_chunks.append(load_chunk(c))
+
+        bias_rows = keep.tile([P, P], BF16)
+        nc.sync.dma_start(
+            out=bias_rows[:],
+            in_=conv_b.rearrange("(o h d) -> o h d", o=1, h=HALVES).broadcast_to([SEQS, HALVES, P]),
+        )
+
+        identity = keep.tile([P, P], F32)
+        masks.make_identity(nc, identity[:])
+        warm = keep.tile([P, 1], F32)
+        nc.vector.memset(warm[:], 0.0)
+        nc.scalar.activation(out=warm[:], in_=warm[:], func=ACT.Exp)
+
+        best = keep.tile([P, SEQS, HALVES], F32)
+
+        for c in range(CHUNKS):
+            x_words = x_chunks[c][:].bitcast(F32)
+            flipped = psum_t.tile([P, ROWS_PER_PARTITION * PAIRS, P], F32)
+            for t in range(ROWS_PER_PARTITION):
+                for u in range(PAIRS):
+                    nc.tensor.transpose(
+                        flipped[:, t * PAIRS + u, :],
+                        x_words[:, t * WORDS_PER_ROW + u : (t + 1) * WORDS_PER_ROW : PAIRS],
+                        identity[:],
+                    )
+            grouped = stage.tile([P, CHUNK_ROWS * PACK], BF16, align_bytes=64)
+            nc.scalar.copy(
+                out=grouped[:].bitcast(F32).rearrange("p (r q) -> p r q", q=ROWS_PER_PARTITION * PAIRS),
+                in_=flipped[:].rearrange("p q r -> p r q"),
+            )
+            x_codes = stage.tile([P, CHUNK_ROWS], U32, align_bytes=64)
+            x_scales = stage.tile([P, CHUNK_ROWS], U8, align_bytes=64)
+            nc.vector.quantize_mx(out=x_codes[:].bitcast(FP8X4), scales=x_scales[:], in_=grouped[:])
+            sums = psum_z.tile([P, HALVES, CHUNK_ROWS], F32)
+            for h in range(HALVES):
+                nc.tensor.matmul_mx(
+                    out=sums[:, h, :],
+                    lhsT=w_words[:, 2 * P * h : 2 * P * (h + 1)].bitcast(FP4X4),
+                    lhsT_scale=w_scales[:, P * h : P * (h + 1)],
+                    rhs=x_codes[:].bitcast(FP8X4),
+                    rhs_scale=x_scales[:],
+                    start=True,
+                    stop=True,
+                )
+            nc.vector.tensor_reduce(
+                out=best[:, c * CHUNK_SEQS : (c + 1) * CHUNK_SEQS, :].rearrange("d b h -> d h b"),
+                in_=sums[:].rearrange("d h (b l) -> d h b l", l=POSITIONS),
+                axis=mybir.AxisListType.X,
+                op=ALU.max,
+            )
+
+        best_rows = psum_end.tile([P, P], F32)
+        nc.tensor.transpose(best_rows[:], best[:].rearrange("d b h -> d (b h)"), identity[:])
+        biased = keep.tile([P, P], F32)
+        nc.vector.tensor_tensor(out=biased[:], in0=best_rows[:], in1=bias_rows[:], op=ALU.add)
+        negative = keep.tile([P, P], F32)
+        nc.vector.tensor_scalar(out=negative[:], in0=biased[:], scalar1=0.0, scalar2=None, op0=ALU.min)
+        grown = keep.tile([P, P], F32)
+        nc.scalar.activation(out=grown[:], in_=negative[:], func=ACT.Exp)
+        result = keep.tile([P, P], F32)
+        nc.vector.scalar_tensor_tensor(
+            out=result[:], in0=grown[:], scalar=-1.0, in1=biased[:], op0=ALU.add, op1=ALU.max
+        )
+        nc.sync.dma_start(out=out.rearrange("b (h d) -> (b h) d", h=HALVES), in_=result[:])

@@ -28,6 +28,7 @@ ROWS_PER_PARTITION = BANK_F32 // WORDS_PER_ROW
 CHUNK_ROWS = P * ROWS_PER_PARTITION
 CHUNKS = ROWS // CHUNK_ROWS
 CHUNK_SEQS = CHUNK_ROWS // POSITIONS
+LAG = 2
 SCALE_ROWS_PER_QUADRANT = 4
 
 FLOPS = 2 * ROWS * FEATURES * CHANNELS
@@ -40,9 +41,10 @@ def tile_conceptembedmodel_pa_s_kernel(tc, x, conv_w_words, conv_w_scales, conv_
     x_rows = x.rearrange("b l f -> (b l) f")
 
     with ExitStack() as ctx:
+        ctx.enter_context(tc.manual_schedule())
         keep = ctx.enter_context(tc.tile_pool(name="keep", bufs=1))
         loads = ctx.enter_context(tc.tile_pool(name="loads", bufs=CHUNKS))
-        stage = ctx.enter_context(tc.tile_pool(name="stage", bufs=3))
+        stage = ctx.enter_context(tc.tile_pool(name="stage", bufs=LAG + 2))
         psum_t = ctx.enter_context(tc.psum_pool(name="psum_t", bufs=3))
         psum_z = ctx.enter_context(tc.psum_pool(name="psum_z", bufs=3))
         psum_end = ctx.enter_context(tc.psum_pool(name="psum_end", bufs=1))
@@ -87,7 +89,10 @@ def tile_conceptembedmodel_pa_s_kernel(tc, x, conv_w_words, conv_w_scales, conv_
 
         best = keep.tile([P, SEQS, HALVES], F32)
 
-        for c in range(CHUNKS):
+        grouped_of = {}
+        codes_of = {}
+
+        def transpose_chunk(c):
             x_words = x_chunks[c][:].bitcast(F32)
             flipped = psum_t.tile([P, ROWS_PER_PARTITION * PAIRS, P], F32)
             for t in range(ROWS_PER_PARTITION):
@@ -102,9 +107,18 @@ def tile_conceptembedmodel_pa_s_kernel(tc, x, conv_w_words, conv_w_scales, conv_
                 out=grouped[:].bitcast(F32).rearrange("p (r q) -> p r q", q=ROWS_PER_PARTITION * PAIRS),
                 in_=flipped[:].rearrange("p q r -> p r q"),
             )
+            grouped_of[c] = grouped
+
+        def quantise_chunk(c):
             x_codes = stage.tile([P, CHUNK_ROWS], U32, align_bytes=64)
             x_scales = stage.tile([P, CHUNK_ROWS], U8, align_bytes=64)
-            nc.vector.quantize_mx(out=x_codes[:].bitcast(FP8X4), scales=x_scales[:], in_=grouped[:])
+            nc.vector.quantize_mx(
+                out=x_codes[:].bitcast(FP8X4), scales=x_scales[:], in_=grouped_of[c][:]
+            )
+            codes_of[c] = (x_codes, x_scales)
+
+        def multiply_chunk(c):
+            x_codes, x_scales = codes_of[c]
             sums = psum_z.tile([P, HALVES, CHUNK_ROWS], F32)
             for h in range(HALVES):
                 nc.tensor.matmul_mx(
@@ -122,6 +136,14 @@ def tile_conceptembedmodel_pa_s_kernel(tc, x, conv_w_words, conv_w_scales, conv_
                 axis=mybir.AxisListType.X,
                 op=ALU.max,
             )
+
+        for c in range(CHUNKS + LAG):
+            if c < CHUNKS:
+                transpose_chunk(c)
+            if c >= LAG:
+                multiply_chunk(c - LAG)
+            if c < CHUNKS:
+                quantise_chunk(c)
 
         best_rows = psum_end.tile([P, P], F32)
         nc.tensor.transpose(best_rows[:], best[:].rearrange("d b h -> d (b h)"), identity[:])

@@ -149,12 +149,14 @@ def tile_conceptembedmodel_pa_s_kernel(tc, x, conv_w_words, conv_w_scales, conv_
         nc.tensor.transpose(best_rows[:], best[:].rearrange("d b h -> d (b h)"), identity[:])
         biased = keep.tile([P, P], F32)
         nc.vector.tensor_tensor(out=biased[:], in0=best_rows[:], in1=bias_rows[:], op=ALU.add)
-        negative = keep.tile([P, P], F32)
-        nc.vector.tensor_scalar(out=negative[:], in0=biased[:], scalar1=0.0, scalar2=None, op0=ALU.min)
         grown = keep.tile([P, P], F32)
-        nc.scalar.activation(out=grown[:], in_=negative[:], func=ACT.Exp)
+        nc.scalar.activation(out=grown[:], in_=biased[:], func=ACT.Exp)
+        straight = keep.tile([P, P], F32)
+        nc.vector.tensor_scalar(
+            out=straight[:], in0=biased[:], scalar1=0.0, scalar2=-1.0, op0=ALU.max, op1=ALU.add
+        )
         result = keep.tile([P, P], F32)
         nc.vector.scalar_tensor_tensor(
-            out=result[:], in0=grown[:], scalar=-1.0, in1=biased[:], op0=ALU.add, op1=ALU.max
+            out=result[:], in0=grown[:], scalar=1.0, in1=straight[:], op0=ALU.min, op1=ALU.add
         )
         nc.sync.dma_start(out=out.rearrange("b (h d) -> (b h) d", h=HALVES), in_=result[:])

@@ -30,6 +30,7 @@ CHUNKS = ROWS // CHUNK_ROWS
 CHUNK_SEQS = CHUNK_ROWS // POSITIONS
 LAG = 2
 SCALE_ROWS_PER_QUADRANT = 4
+WARM_UPS = 4
 
 FLOPS = 2 * ROWS * FEATURES * CHANNELS
 
@@ -48,6 +49,12 @@ def tile_conceptembedmodel_pa_s_kernel(tc, x, conv_w_words, conv_w_scales, conv_
         psum_t = ctx.enter_context(tc.psum_pool(name="psum_t", bufs=3))
         psum_z = ctx.enter_context(tc.psum_pool(name="psum_z", bufs=3))
         psum_end = ctx.enter_context(tc.psum_pool(name="psum_end", bufs=1))
+
+        spin = keep.tile([P, P], F32)
+        nc.gpsimd.memset(spin[:], 0.0)
+        spun = psum_end.tile([P, P], F32)
+        for _ in range(WARM_UPS):
+            nc.tensor.matmul(spun[:], lhsT=spin[:], rhs=spin[:], start=True, stop=True)
 
         def load_chunk(c):
             x_chunk = loads.tile([P, ROWS_PER_PARTITION * FEATURES], BF16)

@@ -28,7 +28,6 @@ ROWS_PER_PARTITION = BANK_F32 // WORDS_PER_ROW
 CHUNK_ROWS = P * ROWS_PER_PARTITION
 CHUNKS = ROWS // CHUNK_ROWS
 CHUNK_SEQS = CHUNK_ROWS // POSITIONS
-LAG = 2
 SCALE_ROWS_PER_QUADRANT = 4
 WARM_UPS = 4
 
@@ -45,7 +44,7 @@ def tile_conceptembedmodel_pa_s_kernel(tc, x, conv_w_words, conv_w_scales, conv_
         ctx.enter_context(tc.manual_schedule())
         keep = ctx.enter_context(tc.tile_pool(name="keep", bufs=1))
         loads = ctx.enter_context(tc.tile_pool(name="loads", bufs=CHUNKS))
-        stage = ctx.enter_context(tc.tile_pool(name="stage", bufs=LAG + 2))
+        stage = ctx.enter_context(tc.tile_pool(name="stage", bufs=5))
         psum_t = ctx.enter_context(tc.psum_pool(name="psum_t", bufs=3))
         psum_z = ctx.enter_context(tc.psum_pool(name="psum_z", bufs=3))
         psum_end = ctx.enter_context(tc.psum_pool(name="psum_end", bufs=1))
@@ -98,6 +97,7 @@ def tile_conceptembedmodel_pa_s_kernel(tc, x, conv_w_words, conv_w_scales, conv_
 
         grouped_of = {}
         codes_of = {}
+        sums_of = {}
 
         def transpose_chunk(c):
             x_words = x_chunks[c][:].bitcast(F32)
@@ -137,6 +137,10 @@ def tile_conceptembedmodel_pa_s_kernel(tc, x, conv_w_words, conv_w_scales, conv_
                     start=True,
                     stop=True,
                 )
+            sums_of[c] = sums
+
+        def reduce_chunk(c):
+            sums = sums_of[c]
             nc.vector.tensor_reduce(
                 out=best[:, c * CHUNK_SEQS : (c + 1) * CHUNK_SEQS, :].rearrange("d b h -> d h b"),
                 in_=sums[:].rearrange("d h (b l) -> d h b l", l=POSITIONS),
@@ -144,13 +148,25 @@ def tile_conceptembedmodel_pa_s_kernel(tc, x, conv_w_words, conv_w_scales, conv_
                 op=ALU.max,
             )
 
-        for c in range(CHUNKS + LAG):
-            if c < CHUNKS:
-                transpose_chunk(c)
-            if c >= LAG:
-                multiply_chunk(c - LAG)
-            if c < CHUNKS:
-                quantise_chunk(c)
+        def in_range(c):
+            return 0 <= c < CHUNKS
+
+        transpose_chunk(0)
+        quantise_chunk(0)
+        for first in range(1, CHUNKS + 2, 2):
+            for c in (first, first + 1):
+                if in_range(c):
+                    transpose_chunk(c)
+            for c in (first - 2, first - 1):
+                if in_range(c):
+                    multiply_chunk(c)
+            if in_range(first):
+                quantise_chunk(first)
+            for c in (first - 2, first - 1):
+                if in_range(c):
+                    reduce_chunk(c)
+            if in_range(first + 1):
+                quantise_chunk(first + 1)
 
         best_rows = psum_end.tile([P, P], F32)
         nc.tensor.transpose(best_rows[:], best[:].rearrange("d b h -> d (b h)"), identity[:])

@@ -29,6 +29,10 @@ CHUNK_ROWS = P * ROWS_PER_PARTITION
 CHUNKS = ROWS // CHUNK_ROWS
 CHUNK_SEQS = CHUNK_ROWS // POSITIONS
 SCALE_ROWS_PER_QUADRANT = 4
+ORDER = (
+    "T0 T1 T2 T3 Q0 Q1 M0 M1 Q2 R0 Q3 R1 "
+    "T4 T5 T6 T7 M2 M3 Q4 M4 Q5 Q6 R2 M5 R3 M6 Q7 R4 M7 R5 R6 R7"
+)
 WARM_UPS = 4
 
 FLOPS = 2 * ROWS * FEATURES * CHANNELS
@@ -44,16 +48,16 @@ def tile_conceptembedmodel_pa_s_kernel(tc, x, conv_w_words, conv_w_scales, conv_
         ctx.enter_context(tc.manual_schedule())
         keep = ctx.enter_context(tc.tile_pool(name="keep", bufs=1))
         loads = ctx.enter_context(tc.tile_pool(name="loads", bufs=CHUNKS))
-        stage = ctx.enter_context(tc.tile_pool(name="stage", bufs=5))
-        psum_t = ctx.enter_context(tc.psum_pool(name="psum_t", bufs=3))
+        stage = ctx.enter_context(tc.tile_pool(name="stage", bufs=CHUNKS))
+        psum_t = ctx.enter_context(tc.psum_pool(name="psum_t", bufs=4))
         psum_z = ctx.enter_context(tc.psum_pool(name="psum_z", bufs=3))
         psum_end = ctx.enter_context(tc.psum_pool(name="psum_end", bufs=1))
 
         spin = keep.tile([P, P], F32)
         nc.gpsimd.memset(spin[:], 0.0)
-        spun = psum_end.tile([P, P], F32)
+        best_rows = psum_end.tile([P, P], F32)
         for _ in range(WARM_UPS):
-            nc.tensor.matmul(spun[:], lhsT=spin[:], rhs=spin[:], start=True, stop=True)
+            nc.tensor.matmul(best_rows[:], lhsT=spin[:], rhs=spin[:], start=True, stop=True)
 
         def load_chunk(c):
             x_chunk = loads.tile([P, ROWS_PER_PARTITION * FEATURES], BF16)
@@ -148,27 +152,10 @@ def tile_conceptembedmodel_pa_s_kernel(tc, x, conv_w_words, conv_w_scales, conv_
                 op=ALU.max,
             )
 
-        def in_range(c):
-            return 0 <= c < CHUNKS
+        steps = {"T": transpose_chunk, "Q": quantise_chunk, "M": multiply_chunk, "R": reduce_chunk}
+        for step in ORDER.split():
+            steps[step[0]](int(step[1:]))
 
-        transpose_chunk(0)
-        quantise_chunk(0)
-        for first in range(1, CHUNKS + 2, 2):
-            for c in (first, first + 1):
-                if in_range(c):
-                    transpose_chunk(c)
-            for c in (first - 2, first - 1):
-                if in_range(c):
-                    multiply_chunk(c)
-            if in_range(first):
-                quantise_chunk(first)
-            for c in (first - 2, first - 1):
-                if in_range(c):
-                    reduce_chunk(c)
-            if in_range(first + 1):
-                quantise_chunk(first + 1)
-
-        best_rows = psum_end.tile([P, P], F32)
         nc.tensor.transpose(best_rows[:], best[:].rearrange("d b h -> d (b h)"), identity[:])
         biased = keep.tile([P, P], F32)
         nc.vector.tensor_tensor(out=biased[:], in0=best_rows[:], in1=bias_rows[:], op=ALU.add)

@@ -33,6 +33,7 @@ ORDER = (
     "T0 T1 T2 T3 Q0 Q1 M0 M1 Q2 R0 Q3 R1 "
     "T4 T5 T6 T7 M2 M3 Q4 M4 Q5 Q6 R2 M5 R3 M6 Q7 R4 M7 R5 R6 R7"
 )
+FIRST_RUN = 4
 WARM_UPS = 4
 
 FLOPS = 2 * ROWS * FEATURES * CHANNELS
@@ -69,7 +70,9 @@ def tile_conceptembedmodel_pa_s_kernel(tc, x, conv_w_words, conv_w_scales, conv_
             )
             return x_chunk
 
-        x_chunks = [load_chunk(0), load_chunk(1)]
+        x_chunks = []
+        for c in range(FIRST_RUN):
+            x_chunks.append(load_chunk(c))
 
         w_words = keep.tile([P, 2 * CHANNELS], U8, align_bytes=64)
         nc.sync.dma_start(out=w_words[:].bitcast(I32), in_=conv_w_words[0].bitcast(I32))
@@ -82,7 +85,7 @@ def tile_conceptembedmodel_pa_s_kernel(tc, x, conv_w_words, conv_w_scales, conv_
                 in_=conv_w_scales[0, first : first + SCALE_ROWS_PER_QUADRANT, :].bitcast(I32),
             )
 
-        for c in range(2, CHUNKS):
+        for c in range(FIRST_RUN, CHUNKS):
             x_chunks.append(load_chunk(c))
 
         bias_rows = keep.tile([P, P], BF16)

@@ -14,26 +14,17 @@ ALU = mybir.AluOpType
 ACT = mybir.ActivationFunctionType
 
 P = 128
-PACK = 4
-SEQS = 64
-POSITIONS = 32
-FEATURES = 512
-CHANNELS = 256
+SEQS, POSITIONS, FEATURES, CHANNELS = 64, 32, 512, 256
 ROWS = SEQS * POSITIONS
 HALVES = CHANNELS // P
 WORDS_PER_ROW = FEATURES // 2
-PAIRS = PACK // 2
-BANK_F32 = 512
-ROWS_PER_PARTITION = BANK_F32 // WORDS_PER_ROW
-CHUNK_ROWS = P * ROWS_PER_PARTITION
-CHUNKS = ROWS // CHUNK_ROWS
-CHUNK_SEQS = CHUNK_ROWS // POSITIONS
-SCALE_ROWS_PER_QUADRANT = 4
+PIECES = [256,256,256,256,256,256,256,256]
+LOADS = "0 1 2 3 W S 4 5 6 7 B"
 ORDER = (
-    "T0 T1 T2 T3 Q0 Q1 M0 M1 Q2 R0 Q3 R1 "
-    "T4 T5 T6 T7 M2 M3 Q4 M4 Q5 Q6 R2 M5 R3 M6 Q7 R4 M7 R5 R6 R7"
+    "T0 C0 T1 C1 T2 C2 T3 C3 Q0 M0 Q1 M1 T4 C4 T5 C5 "
+    "Q2 M2 R0 Q3 M3 T6 C6 T7 C7 R1 Q4 B0 M4 R2 Q5 M5 "
+    "R3 Q6 M6 R4 Q7 M7 R5 F0:4 R6 W0 W0 R7 F5:7"
 )
-FIRST_RUN = 4
 WARM_UPS = 4
 
 FLOPS = 2 * ROWS * FEATURES * CHANNELS
@@ -41,99 +32,112 @@ FLOPS = 2 * ROWS * FEATURES * CHANNELS
 
 def tile_conceptembedmodel_pa_s_kernel(tc, x, conv_w_words, conv_w_scales, conv_b, out):
     nc = tc.nc
-    assert tuple(x.shape) == (SEQS, POSITIONS, FEATURES)
-    assert FEATURES == P * PACK, "the contraction is one matmul_mx pass"
     x_rows = x.rearrange("b l f -> (b l) f")
+    first_row = [sum(PIECES[:i]) for i in range(len(PIECES))]
+    assert sum(PIECES) == ROWS
 
     with ExitStack() as ctx:
         ctx.enter_context(tc.manual_schedule())
         keep = ctx.enter_context(tc.tile_pool(name="keep", bufs=1))
-        loads = ctx.enter_context(tc.tile_pool(name="loads", bufs=CHUNKS))
-        stage = ctx.enter_context(tc.tile_pool(name="stage", bufs=CHUNKS))
-        psum_t = ctx.enter_context(tc.psum_pool(name="psum_t", bufs=4))
-        psum_z = ctx.enter_context(tc.psum_pool(name="psum_z", bufs=3))
+        loads = ctx.enter_context(tc.tile_pool(name="loads", bufs=len(PIECES)))
+        stage = ctx.enter_context(tc.tile_pool(name="stage", bufs=len(PIECES)))
+        psum = ctx.enter_context(tc.psum_pool(name="psum", bufs=6))
         psum_end = ctx.enter_context(tc.psum_pool(name="psum_end", bufs=1))
 
         spin = keep.tile([P, P], F32)
         nc.gpsimd.memset(spin[:], 0.0)
-        best_rows = psum_end.tile([P, P], F32)
+        end_a = psum_end.tile([P, P], F32)
+        end_b = psum_end.tile([P, P], F32)
+
+        def dummy():
+            nc.tensor.matmul(end_a[:], lhsT=spin[:], rhs=spin[:], start=True, stop=True)
+
         for _ in range(WARM_UPS):
-            nc.tensor.matmul(best_rows[:], lhsT=spin[:], rhs=spin[:], start=True, stop=True)
+            dummy()
 
-        def load_chunk(c):
-            x_chunk = loads.tile([P, ROWS_PER_PARTITION * FEATURES], BF16)
-            nc.sync.dma_start(
-                out=x_chunk[:],
-                in_=x_rows[c * CHUNK_ROWS : (c + 1) * CHUNK_ROWS, :].rearrange(
-                    "(r t) f -> r (t f)", t=ROWS_PER_PARTITION
-                ),
-            )
-            return x_chunk
-
-        x_chunks = []
-        for c in range(FIRST_RUN):
-            x_chunks.append(load_chunk(c))
-
+        x_of = {}
         w_words = keep.tile([P, 2 * CHANNELS], U8, align_bytes=64)
-        nc.sync.dma_start(out=w_words[:].bitcast(I32), in_=conv_w_words[0].bitcast(I32))
         w_scales = keep.tile([P, CHANNELS], U8, align_bytes=64)
-        nc.vector.memset(w_scales[:].bitcast(I32), 0)
-        for quadrant in range(P // 32):
-            first = SCALE_ROWS_PER_QUADRANT * quadrant
-            nc.sync.dma_start(
-                out=w_scales[32 * quadrant : 32 * quadrant + SCALE_ROWS_PER_QUADRANT, :].bitcast(I32),
-                in_=conv_w_scales[0, first : first + SCALE_ROWS_PER_QUADRANT, :].bitcast(I32),
-            )
-
-        for c in range(FIRST_RUN, CHUNKS):
-            x_chunks.append(load_chunk(c))
-
         bias_rows = keep.tile([P, P], BF16)
-        nc.sync.dma_start(
-            out=bias_rows[:],
-            in_=conv_b.rearrange("(o h d) -> o h d", o=1, h=HALVES).broadcast_to([SEQS, HALVES, P]),
-        )
+        nc.vector.memset(w_scales[:].bitcast(I32), 0)
+
+        def load(what):
+            if what == "W":
+                nc.sync.dma_start(out=w_words[:].bitcast(I32), in_=conv_w_words[0].bitcast(I32))
+            elif what == "S":
+                for quadrant in range(4):
+                    nc.sync.dma_start(
+                        out=w_scales[32 * quadrant : 32 * quadrant + 4, :].bitcast(I32),
+                        in_=conv_w_scales[0, 4 * quadrant : 4 * quadrant + 4, :].bitcast(I32),
+                    )
+            elif what == "B":
+                nc.sync.dma_start(
+                    out=bias_rows[:],
+                    in_=conv_b.rearrange("(o h d) -> o h d", o=1, h=HALVES).broadcast_to([SEQS, HALVES, P]),
+                )
+            else:
+                i = int(what)
+                t = PIECES[i] // P
+                x_piece = loads.tile([P, t * FEATURES], BF16)
+                nc.sync.dma_start(
+                    out=x_piece[:],
+                    in_=x_rows[first_row[i] : first_row[i] + PIECES[i], :].rearrange("(r t) f -> r (t f)", t=t),
+                )
+                x_of[i] = x_piece
+
+        for what in LOADS.split():
+            load(what)
 
         identity = keep.tile([P, P], F32)
         masks.make_identity(nc, identity[:])
+        identity_bf = keep.tile([P, P], BF16)
+        nc.gpsimd.tensor_copy(out=identity_bf[:], in_=identity[:])
+        minus_one = keep.tile([P, P], BF16)
+        nc.gpsimd.memset(minus_one[:], -1.0)
+        minus_bias = keep.tile([P, SEQS, HALVES], F32)
+        floored = keep.tile([P, SEQS, HALVES], F32)
         warm = keep.tile([P, 1], F32)
         nc.vector.memset(warm[:], 0.0)
         nc.scalar.activation(out=warm[:], in_=warm[:], func=ACT.Exp)
 
         best = keep.tile([P, SEQS, HALVES], F32)
+        flipped_of, grouped_of, codes_of, sums_of = {}, {}, {}, {}
 
-        grouped_of = {}
-        codes_of = {}
-        sums_of = {}
-
-        def transpose_chunk(c):
-            x_words = x_chunks[c][:].bitcast(F32)
-            flipped = psum_t.tile([P, ROWS_PER_PARTITION * PAIRS, P], F32)
-            for t in range(ROWS_PER_PARTITION):
-                for u in range(PAIRS):
+        def transpose(i):
+            t_n = PIECES[i] // P
+            x_words = x_of[i][:].bitcast(F32)
+            bank = psum.tile([P, 512], F32)
+            flipped = bank[:, : t_n * 2 * P].rearrange("p (q r) -> p q r", q=t_n * 2)
+            for t in range(t_n):
+                for u in range(2):
                     nc.tensor.transpose(
-                        flipped[:, t * PAIRS + u, :],
-                        x_words[:, t * WORDS_PER_ROW + u : (t + 1) * WORDS_PER_ROW : PAIRS],
+                        flipped[:, t * 2 + u, :],
+                        x_words[:, t * WORDS_PER_ROW + u : (t + 1) * WORDS_PER_ROW : 2],
                         identity[:],
                     )
-            grouped = stage.tile([P, CHUNK_ROWS * PACK], BF16, align_bytes=64)
-            nc.scalar.copy(
-                out=grouped[:].bitcast(F32).rearrange("p (r q) -> p r q", q=ROWS_PER_PARTITION * PAIRS),
-                in_=flipped[:].rearrange("p q r -> p r q"),
-            )
-            grouped_of[c] = grouped
+            flipped_of[i] = flipped
 
-        def quantise_chunk(c):
-            x_codes = stage.tile([P, CHUNK_ROWS], U32, align_bytes=64)
-            x_scales = stage.tile([P, CHUNK_ROWS], U8, align_bytes=64)
-            nc.vector.quantize_mx(
-                out=x_codes[:].bitcast(FP8X4), scales=x_scales[:], in_=grouped_of[c][:]
-            )
-            codes_of[c] = (x_codes, x_scales)
+        def group(i, on_vector):
+            q = PIECES[i] // P * 2
+            grouped = stage.tile([P, PIECES[i] * 4], BF16, align_bytes=64)
+            target = grouped[:].bitcast(F32).rearrange("p (r q) -> p r q", q=q)
+            source = flipped_of[i].rearrange("p q r -> p r q")
+            if on_vector:
+                nc.vector.tensor_copy(out=target, in_=source)
+            else:
+                nc.scalar.copy(out=target, in_=source)
+            grouped_of[i] = grouped
 
-        def multiply_chunk(c):
-            x_codes, x_scales = codes_of[c]
-            sums = psum_z.tile([P, HALVES, CHUNK_ROWS], F32)
+        def quantise(i):
+            x_codes = stage.tile([P, PIECES[i]], U32, align_bytes=64)
+            x_scales = stage.tile([P, PIECES[i]], U8, align_bytes=64)
+            nc.vector.quantize_mx(out=x_codes[:].bitcast(FP8X4), scales=x_scales[:], in_=grouped_of[i][:])
+            codes_of[i] = (x_codes, x_scales)
+
+        def multiply(i):
+            x_codes, x_scales = codes_of[i]
+            bank = psum.tile([P, 512], F32)
+            sums = bank[:, : HALVES * PIECES[i]].rearrange("p (h r) -> p h r", h=HALVES)
             for h in range(HALVES):
                 nc.tensor.matmul_mx(
                     out=sums[:, h, :],
@@ -144,32 +148,72 @@ def tile_conceptembedmodel_pa_s_kernel(tc, x, conv_w_words, conv_w_scales, conv_
                     start=True,
                     stop=True,
                 )
-            sums_of[c] = sums
+            sums_of[i] = sums
 
-        def reduce_chunk(c):
-            sums = sums_of[c]
+        def reduce(i):
+            b0 = first_row[i] // POSITIONS
+            b1 = b0 + PIECES[i] // POSITIONS
             nc.vector.tensor_reduce(
-                out=best[:, c * CHUNK_SEQS : (c + 1) * CHUNK_SEQS, :].rearrange("d b h -> d h b"),
-                in_=sums[:].rearrange("d h (b l) -> d h b l", l=POSITIONS),
+                out=best[:, b0:b1, :].rearrange("d b h -> d h b"),
+                in_=sums_of[i].rearrange("d h (b l) -> d h b l", l=POSITIONS),
                 axis=mybir.AxisListType.X,
                 op=ALU.max,
             )
 
-        steps = {"T": transpose_chunk, "Q": quantise_chunk, "M": multiply_chunk, "R": reduce_chunk}
-        for step in ORDER.split():
-            steps[step[0]](int(step[1:]))
+        def bias():
+            turned = psum.tile([P, P], F32, name="bank")
+            nc.tensor.matmul(turned[:], lhsT=bias_rows[:], rhs=identity_bf[:], start=True, stop=True)
+            for end in (end_a, end_b):
+                nc.tensor.matmul(end[:], lhsT=identity_bf[:], rhs=bias_rows[:], start=True, stop=False)
+            nc.tensor.matmul(end_b[:], lhsT=identity_bf[:], rhs=minus_one[:], start=False, stop=False)
+            nc.scalar.activation(
+                out=minus_bias[:].rearrange("d b h -> d (b h)"), in_=turned[:], func=ACT.Copy, scale=-1.0
+            )
 
-        nc.tensor.transpose(best_rows[:], best[:].rearrange("d b h -> d (b h)"), identity[:])
-        biased = keep.tile([P, P], F32)
-        nc.vector.tensor_tensor(out=biased[:], in0=best_rows[:], in1=bias_rows[:], op=ALU.add)
-        grown = keep.tile([P, P], F32)
-        nc.scalar.activation(out=grown[:], in_=biased[:], func=ACT.Exp)
-        straight = keep.tile([P, P], F32)
-        nc.vector.tensor_scalar(
-            out=straight[:], in0=biased[:], scalar1=0.0, scalar2=-1.0, op0=ALU.max, op1=ALU.add
+        def floor(i, j):
+            b = slice(first_row[i] // POSITIONS, (first_row[j] + PIECES[j]) // POSITIONS)
+            nc.vector.tensor_tensor(
+                out=floored[:, b, :], in0=best[:, b, :], in1=minus_bias[:, b, :], op=ALU.max
+            )
+
+        for step in ORDER.split():
+            kind = step[0]
+            if kind == "T":
+                transpose(int(step[1:]))
+            elif kind == "C":
+                group(int(step[1:]), False)
+            elif kind == "V":
+                group(int(step[1:]), True)
+            elif kind == "Q":
+                quantise(int(step[1:]))
+            elif kind == "M":
+                multiply(int(step[1:]))
+            elif kind == "R":
+                reduce(int(step[1:]))
+            elif kind == "B":
+                bias()
+            elif kind == "F":
+                floor(*[int(v) for v in step[1:].split(":")])
+            elif kind == "W":
+                busy = psum.tile([P, 80], F32, name="bank")
+                nc.tensor.matmul(
+                    busy[:], lhsT=spin[:], rhs=floored[:, 0:40, :].rearrange("d b h -> d (b h)"), start=True, stop=True
+                )
+            else:
+                dummy()
+
+        nc.tensor.matmul(
+            end_a[:], lhsT=best[:].rearrange("d b h -> d (b h)"), rhs=identity[:],
+            is_transpose=True, start=False, stop=True,
         )
+        nc.tensor.matmul(
+            end_b[:], lhsT=floored[:].rearrange("d b h -> d (b h)"), rhs=identity[:],
+            is_transpose=True, start=False, stop=True,
+        )
+        grown = keep.tile([P, P], F32)
+        nc.scalar.activation(out=grown[:], in_=end_a[:], func=ACT.Exp)
         result = keep.tile([P, P], F32)
         nc.vector.scalar_tensor_tensor(
-            out=result[:], in0=grown[:], scalar=1.0, in1=straight[:], op0=ALU.min, op1=ALU.add
+            out=result[:], in0=grown[:], scalar=1.0, in1=end_b[:], op0=ALU.min, op1=ALU.add
         )
         nc.sync.dma_start(out=out.rearrange("b (h d) -> (b h) d", h=HALVES), in_=result[:])

@@ -22,8 +22,8 @@ PIECES = [256,256,256,256,256,256,256,256]
 LOADS = "0 1 2 3 W S 4 5 6 7 B"
 ORDER = (
     "T0 C0 T1 C1 T2 C2 T3 C3 Q0 M0 Q1 M1 T4 C4 T5 C5 "
-    "Q2 M2 R0 Q3 M3 T6 C6 T7 C7 R1 Q4 B0 M4 R2 Q5 M5 "
-    "R3 Q6 M6 R4 Q7 M7 R5 F0:4 R6 W0 W0 R7 F5:7"
+    "Q2 M2 R0 Q3 M3 T6 C6 T7 C7 R1 Q4 M4 R2 Q5 M5 R3 "
+    "Q6 M6 B0 R4 Q7 M7 R5 R6 F0:6 W5 W6 R7 F7:7"
 )
 WARM_UPS = 4
 
@@ -94,7 +94,7 @@ def tile_conceptembedmodel_pa_s_kernel(tc, x, conv_w_words, conv_w_scales, conv_
         nc.gpsimd.tensor_copy(out=identity_bf[:], in_=identity[:])
         minus_one = keep.tile([P, P], BF16)
         nc.gpsimd.memset(minus_one[:], -1.0)
-        minus_bias = keep.tile([P, SEQS, HALVES], F32)
+        bias_columns = keep.tile([P, HALVES], F32)
         floored = keep.tile([P, SEQS, HALVES], F32)
         warm = keep.tile([P, 1], F32)
         nc.vector.memset(warm[:], 0.0)
@@ -163,18 +163,16 @@ def tile_conceptembedmodel_pa_s_kernel(tc, x, conv_w_words, conv_w_scales, conv_
         def bias():
             turned = psum.tile([P, P], F32, name="bank")
             nc.tensor.matmul(turned[:], lhsT=bias_rows[:], rhs=identity_bf[:], start=True, stop=True)
-            for end in (end_a, end_b):
-                nc.tensor.matmul(end[:], lhsT=identity_bf[:], rhs=bias_rows[:], start=True, stop=False)
-            nc.tensor.matmul(end_b[:], lhsT=identity_bf[:], rhs=minus_one[:], start=False, stop=False)
-            nc.scalar.activation(
-                out=minus_bias[:].rearrange("d b h -> d (b h)"), in_=turned[:], func=ACT.Copy, scale=-1.0
-            )
+            nc.tensor.matmul(end_a[:], lhsT=identity_bf[:], rhs=bias_rows[:], start=True, stop=False)
+            nc.tensor.matmul(end_b[:], lhsT=identity_bf[:], rhs=minus_one[:], start=True, stop=False)
+            nc.scalar.copy(out=bias_columns[:], in_=turned[:, 0:HALVES])
 
         def floor(i, j):
             b = slice(first_row[i] // POSITIONS, (first_row[j] + PIECES[j]) // POSITIONS)
-            nc.vector.tensor_tensor(
-                out=floored[:, b, :], in0=best[:, b, :], in1=minus_bias[:, b, :], op=ALU.max
-            )
+            for h in range(HALVES):
+                nc.scalar.activation(
+                    out=floored[:, b, h], in_=best[:, b, h], func=ACT.Relu, bias=bias_columns[:, h : h + 1]
+                )
 
         for step in ORDER.split():
             kind = step[0]
@@ -195,9 +193,10 @@ def tile_conceptembedmodel_pa_s_kernel(tc, x, conv_w_words, conv_w_scales, conv_
             elif kind == "F":
                 floor(*[int(v) for v in step[1:].split(":")])
             elif kind == "W":
-                busy = psum.tile([P, 80], F32, name="bank")
+                seen = (first_row[int(step[1:])] + PIECES[int(step[1:])]) // POSITIONS
+                busy = psum.tile([P, seen * HALVES], F32, name="bank")
                 nc.tensor.matmul(
-                    busy[:], lhsT=spin[:], rhs=floored[:, 0:40, :].rearrange("d b h -> d (b h)"), start=True, stop=True
+                    busy[:], lhsT=spin[:], rhs=best[:, 0:seen, :].rearrange("d b h -> d (b h)"), start=True, stop=True
                 )
             else:
                 dummy()

@@ -23,7 +23,7 @@ LOADS = "0 1 2 3 W S 4 5 6 7 B"
 ORDER = (
     "T0 C0 T1 C1 T2 C2 T3 C3 Q0 M0 Q1 M1 T4 C4 T5 C5 "
     "Q2 M2 R0 Q3 M3 T6 C6 T7 C7 R1 Q4 M4 R2 Q5 M5 R3 "
-    "Q6 M6 B0 R4 Q7 M7 R5 R6 F0:6 W5 W6 R7 F7:7"
+    "Q6 M6 R4 Q7 M7 B0 R5 R6 F0:6 W5 W6 R7 F7:7"
 )
 WARM_UPS = 4
 
@@ -60,6 +60,7 @@ def tile_conceptembedmodel_pa_s_kernel(tc, x, conv_w_words, conv_w_scales, conv_
         w_scales = keep.tile([P, CHANNELS], U8, align_bytes=64)
         bias_rows = keep.tile([P, P], BF16)
         nc.vector.memset(w_scales[:].bitcast(I32), 0)
+        nc.vector.memset(bias_rows[:], 0.0)
 
         def load(what):
             if what == "W":
@@ -71,10 +72,7 @@ def tile_conceptembedmodel_pa_s_kernel(tc, x, conv_w_words, conv_w_scales, conv_
                         in_=conv_w_scales[0, 4 * quadrant : 4 * quadrant + 4, :].bitcast(I32),
                     )
             elif what == "B":
-                nc.sync.dma_start(
-                    out=bias_rows[:],
-                    in_=conv_b.rearrange("(o h d) -> o h d", o=1, h=HALVES).broadcast_to([SEQS, HALVES, P]),
-                )
+                nc.sync.dma_start(out=bias_rows[0:HALVES, :], in_=conv_b.rearrange("(h d) -> h d", h=HALVES))
             else:
                 i = int(what)
                 t = PIECES[i] // P
@@ -92,6 +90,11 @@ def tile_conceptembedmodel_pa_s_kernel(tc, x, conv_w_words, conv_w_scales, conv_
         masks.make_identity(nc, identity[:])
         identity_bf = keep.tile([P, P], BF16)
         nc.gpsimd.tensor_copy(out=identity_bf[:], in_=identity[:])
+        selector = keep.tile([P, SEQS, HALVES], BF16)
+        nc.gpsimd.tensor_copy(
+            out=selector[:], in_=identity[:, 0:HALVES].rearrange("p (o h) -> p o h", o=1).broadcast_to([P, SEQS, HALVES])
+        )
+        selector_rows = selector[:].rearrange("p b h -> p (b h)")
         minus_one = keep.tile([P, P], BF16)
         nc.gpsimd.memset(minus_one[:], -1.0)
         bias_columns = keep.tile([P, HALVES], F32)
@@ -162,8 +165,8 @@ def tile_conceptembedmodel_pa_s_kernel(tc, x, conv_w_words, conv_w_scales, conv_
 
         def bias():
             turned = psum.tile([P, P], F32, name="bank")
-            nc.tensor.matmul(turned[:], lhsT=bias_rows[:], rhs=identity_bf[:], start=True, stop=True)
-            nc.tensor.matmul(end_a[:], lhsT=identity_bf[:], rhs=bias_rows[:], start=True, stop=False)
+            nc.tensor.matmul(turned[:], lhsT=bias_rows[:], rhs=selector_rows, start=True, stop=True)
+            nc.tensor.matmul(end_a[:], lhsT=selector_rows, rhs=bias_rows[:], start=True, stop=False)
             nc.tensor.matmul(end_b[:], lhsT=identity_bf[:], rhs=minus_one[:], start=True, stop=False)
             nc.scalar.copy(out=bias_columns[:], in_=turned[:, 0:HALVES])
 

@@ -21,9 +21,9 @@ WORDS_PER_ROW = FEATURES // 2
 PIECES = [256,256,256,256,256,256,256,256]
 LOADS = "0 1 2 3 W S 4 5 6 7 B"
 ORDER = (
-    "T0 C0 T1 C1 T2 C2 T3 C3 Q0 M0 Q1 M1 T4 C4 T5 C5 "
-    "Q2 M2 R0 Q3 M3 T6 C6 T7 C7 R1 Q4 M4 R2 Q5 M5 R3 "
-    "Q6 M6 R4 Q7 M7 B0 R5 R6 F0:6 W5 W6 R7 F7:7"
+    "T0 C0 T1 C1 D0 T2 C2 D0 T3 C3 Q0 M0 Q1 M1 T4 C4 "
+    "T5 C5 Q2 M2 R0 Q3 M3 T6 C6 T7 C7 R1 Q4 M4 R2 Q5 "
+    "M5 R3 Q6 M6 R4 Q7 M7 B0 R5 R6 F0:6 W5 W6 R7 F7:7"
 )
 WARM_UPS = 4
 

@@ -21,9 +21,9 @@ WORDS_PER_ROW = FEATURES // 2
 PIECES = [256,256,256,256,256,256,256,256]
 LOADS = "0 1 2 3 W S 4 5 6 7 B"
 ORDER = (
-    "T0 C0 T1 C1 D0 T2 C2 D0 T3 C3 Q0 M0 Q1 M1 T4 C4 "
-    "T5 C5 Q2 M2 R0 Q3 M3 T6 C6 T7 C7 R1 Q4 M4 R2 Q5 "
-    "M5 R3 Q6 M6 R4 Q7 M7 B0 R5 R6 F0:6 W5 W6 R7 F7:7"
+    "T0 C0 T1 C1 D0 T2 C2 T3 C3 Q0 M0 Q1 M1 T4 C4 T5 "
+    "C5 Q2 M2 R0 Q3 M3 T6 C6 T7 C7 R1 Q4 M4 R2 Q5 M5 "
+    "R3 Q6 M6 R4 Q7 M7 B0 R5 R6 F0:6 W5 W6 R7 F7:7"
 )
 WARM_UPS = 4
 

from contextlib import ExitStack

import concourse.masks as masks
import concourse.mybir as mybir

F32 = mybir.dt.float32
BF16 = mybir.dt.bfloat16
I32 = mybir.dt.int32
U32 = mybir.dt.uint32
U8 = mybir.dt.uint8
FP8X4 = mybir.dt.float8_e4m3fn_x4
FP4X4 = mybir.dt.float4_e2m1fn_x4
ALU = mybir.AluOpType
ACT = mybir.ActivationFunctionType

P = 128
SEQS, POSITIONS, FEATURES, CHANNELS = 64, 32, 512, 256
ROWS = SEQS * POSITIONS
HALVES = CHANNELS // P
WORDS_PER_ROW = FEATURES // 2
PIECES = [256,256,256,256,256,256,256,256]
LOADS = "0 1 2 3 W S 4 5 6 7 B"
ORDER = (
    "T0 C0 T1 C1 D0 T2 C2 T3 C3 Q0 M0 Q1 M1 T4 C4 T5 "
    "C5 Q2 M2 R0 Q3 M3 T6 C6 T7 C7 R1 Q4 M4 R2 Q5 M5 "
    "R3 Q6 M6 R4 Q7 M7 B0 R5 R6 F0:6 W5 W6 R7 F7:7"
)
WARM_UPS = 4

FLOPS = 2 * ROWS * FEATURES * CHANNELS


def tile_conceptembedmodel_pa_s_kernel(tc, x, conv_w_words, conv_w_scales, conv_b, out):
    nc = tc.nc
    x_rows = x.rearrange("b l f -> (b l) f")
    first_row = [sum(PIECES[:i]) for i in range(len(PIECES))]
    assert sum(PIECES) == ROWS

    with ExitStack() as ctx:
        ctx.enter_context(tc.manual_schedule())
        keep = ctx.enter_context(tc.tile_pool(name="keep", bufs=1))
        loads = ctx.enter_context(tc.tile_pool(name="loads", bufs=len(PIECES)))
        stage = ctx.enter_context(tc.tile_pool(name="stage", bufs=len(PIECES)))
        psum = ctx.enter_context(tc.psum_pool(name="psum", bufs=6))
        psum_end = ctx.enter_context(tc.psum_pool(name="psum_end", bufs=1))

        spin = keep.tile([P, P], F32)
        nc.gpsimd.memset(spin[:], 0.0)
        end_a = psum_end.tile([P, P], F32)
        end_b = psum_end.tile([P, P], F32)

        def dummy():
            nc.tensor.matmul(end_a[:], lhsT=spin[:], rhs=spin[:], start=True, stop=True)

        for _ in range(WARM_UPS):
            dummy()

        x_of = {}
        w_words = keep.tile([P, 2 * CHANNELS], U8, align_bytes=64)
        w_scales = keep.tile([P, CHANNELS], U8, align_bytes=64)
        bias_rows = keep.tile([P, P], BF16)
        nc.vector.memset(w_scales[:].bitcast(I32), 0)
        nc.vector.memset(bias_rows[:], 0.0)

        def load(what):
            if what == "W":
                nc.sync.dma_start(out=w_words[:].bitcast(I32), in_=conv_w_words[0].bitcast(I32))
            elif what == "S":
                for quadrant in range(4):
                    nc.sync.dma_start(
                        out=w_scales[32 * quadrant : 32 * quadrant + 4, :].bitcast(I32),
                        in_=conv_w_scales[0, 4 * quadrant : 4 * quadrant + 4, :].bitcast(I32),
                    )
            elif what == "B":
                nc.sync.dma_start(out=bias_rows[0:HALVES, :], in_=conv_b.rearrange("(h d) -> h d", h=HALVES))
            else:
                i = int(what)
                t = PIECES[i] // P
                x_piece = loads.tile([P, t * FEATURES], BF16)
                nc.sync.dma_start(
                    out=x_piece[:],
                    in_=x_rows[first_row[i] : first_row[i] + PIECES[i], :].rearrange("(r t) f -> r (t f)", t=t),
                )
                x_of[i] = x_piece

        for what in LOADS.split():
            load(what)

        identity = keep.tile([P, P], F32)
        masks.make_identity(nc, identity[:])
        identity_bf = keep.tile([P, P], BF16)
        nc.gpsimd.tensor_copy(out=identity_bf[:], in_=identity[:])
        selector = keep.tile([P, SEQS, HALVES], BF16)
        nc.gpsimd.tensor_copy(
            out=selector[:], in_=identity[:, 0:HALVES].rearrange("p (o h) -> p o h", o=1).broadcast_to([P, SEQS, HALVES])
        )
        selector_rows = selector[:].rearrange("p b h -> p (b h)")
        minus_one = keep.tile([P, P], BF16)
        nc.gpsimd.memset(minus_one[:], -1.0)
        bias_columns = keep.tile([P, HALVES], F32)
        floored = keep.tile([P, SEQS, HALVES], F32)
        warm = keep.tile([P, 1], F32)
        nc.vector.memset(warm[:], 0.0)
        nc.scalar.activation(out=warm[:], in_=warm[:], func=ACT.Exp)

        best = keep.tile([P, SEQS, HALVES], F32)
        flipped_of, grouped_of, codes_of, sums_of = {}, {}, {}, {}

        def transpose(i):
            t_n = PIECES[i] // P
            x_words = x_of[i][:].bitcast(F32)
            bank = psum.tile([P, 512], F32)
            flipped = bank[:, : t_n * 2 * P].rearrange("p (q r) -> p q r", q=t_n * 2)
            for t in range(t_n):
                for u in range(2):
                    nc.tensor.transpose(
                        flipped[:, t * 2 + u, :],
                        x_words[:, t * WORDS_PER_ROW + u : (t + 1) * WORDS_PER_ROW : 2],
                        identity[:],
                    )
            flipped_of[i] = flipped

        def group(i, on_vector):
            q = PIECES[i] // P * 2
            grouped = stage.tile([P, PIECES[i] * 4], BF16, align_bytes=64)
            target = grouped[:].bitcast(F32).rearrange("p (r q) -> p r q", q=q)
            source = flipped_of[i].rearrange("p q r -> p r q")
            if on_vector:
                nc.vector.tensor_copy(out=target, in_=source)
            else:
                nc.scalar.copy(out=target, in_=source)
            grouped_of[i] = grouped

        def quantise(i):
            x_codes = stage.tile([P, PIECES[i]], U32, align_bytes=64)
            x_scales = stage.tile([P, PIECES[i]], U8, align_bytes=64)
            nc.vector.quantize_mx(out=x_codes[:].bitcast(FP8X4), scales=x_scales[:], in_=grouped_of[i][:])
            codes_of[i] = (x_codes, x_scales)

        def multiply(i):
            x_codes, x_scales = codes_of[i]
            bank = psum.tile([P, 512], F32)
            sums = bank[:, : HALVES * PIECES[i]].rearrange("p (h r) -> p h r", h=HALVES)
            for h in range(HALVES):
                nc.tensor.matmul_mx(
                    out=sums[:, h, :],
                    lhsT=w_words[:, 2 * P * h : 2 * P * (h + 1)].bitcast(FP4X4),
                    lhsT_scale=w_scales[:, P * h : P * (h + 1)],
                    rhs=x_codes[:].bitcast(FP8X4),
                    rhs_scale=x_scales[:],
                    start=True,
                    stop=True,
                )
            sums_of[i] = sums

        def reduce(i):
            b0 = first_row[i] // POSITIONS
            b1 = b0 + PIECES[i] // POSITIONS
            nc.vector.tensor_reduce(
                out=best[:, b0:b1, :].rearrange("d b h -> d h b"),
                in_=sums_of[i].rearrange("d h (b l) -> d h b l", l=POSITIONS),
                axis=mybir.AxisListType.X,
                op=ALU.max,
            )

        def bias():
            turned = psum.tile([P, P], F32, name="bank")
            nc.tensor.matmul(turned[:], lhsT=bias_rows[:], rhs=selector_rows, start=True, stop=True)
            nc.tensor.matmul(end_a[:], lhsT=selector_rows, rhs=bias_rows[:], start=True, stop=False)
            nc.tensor.matmul(end_b[:], lhsT=identity_bf[:], rhs=minus_one[:], start=True, stop=False)
            nc.scalar.copy(out=bias_columns[:], in_=turned[:, 0:HALVES])

        def floor(i, j):
            b = slice(first_row[i] // POSITIONS, (first_row[j] + PIECES[j]) // POSITIONS)
            for h in range(HALVES):
                nc.scalar.activation(
                    out=floored[:, b, h], in_=best[:, b, h], func=ACT.Relu, bias=bias_columns[:, h : h + 1]
                )

        for step in ORDER.split():
            kind = step[0]
            if kind == "T":
                transpose(int(step[1:]))
            elif kind == "C":
                group(int(step[1:]), False)
            elif kind == "V":
                group(int(step[1:]), True)
            elif kind == "Q":
                quantise(int(step[1:]))
            elif kind == "M":
                multiply(int(step[1:]))
            elif kind == "R":
                reduce(int(step[1:]))
            elif kind == "B":
                bias()
            elif kind == "F":
                floor(*[int(v) for v in step[1:].split(":")])
            elif kind == "W":
                seen = (first_row[int(step[1:])] + PIECES[int(step[1:])]) // POSITIONS
                busy = psum.tile([P, seen * HALVES], F32, name="bank")
                nc.tensor.matmul(
                    busy[:], lhsT=spin[:], rhs=best[:, 0:seen, :].rearrange("d b h -> d (b h)"), start=True, stop=True
                )
            else:
                dummy()

        nc.tensor.matmul(
            end_a[:], lhsT=best[:].rearrange("d b h -> d (b h)"), rhs=identity[:],
            is_transpose=True, start=False, stop=True,
        )
        nc.tensor.matmul(
            end_b[:], lhsT=floored[:].rearrange("d b h -> d (b h)"), rhs=identity[:],
            is_transpose=True, start=False, stop=True,
        )
        grown = keep.tile([P, P], F32)
        nc.scalar.activation(out=grown[:], in_=end_a[:], func=ACT.Exp)
        result = keep.tile([P, P], F32)
        nc.vector.scalar_tensor_tensor(
            out=result[:], in0=grown[:], scalar=1.0, in1=end_b[:], op0=ALU.min, op1=ALU.add
        )
        nc.sync.dma_start(out=out.rearrange("b (h d) -> (b h) d", h=HALVES), in_=result[:])
